import numpy as np
import ml_dtypes


def mxq(x, axis, fmt="e4m3"):
    dtype, down = {"e4m3": (ml_dtypes.float8_e4m3fn, 7), "e5m2": (ml_dtypes.float8_e5m2, 14)}[fmt]
    v = np.moveaxis(np.asarray(x, np.float32).astype(ml_dtypes.bfloat16).astype(np.float64), axis, -1)
    blocks = v.reshape(v.shape[:-1] + (-1, 32))
    amax = np.abs(blocks).max(-1, keepdims=True)
    byte = np.maximum(np.where(amax > 0, np.frexp(amax)[1] - 1 + 127, 0) - down, 1)
    scale = np.exp2(byte - 127.0)
    codes = (blocks / scale).astype(np.float32).astype(dtype).astype(np.float64)
    return np.moveaxis((codes * scale).reshape(v.shape), -1, axis)


WIDE = False


def mx_kscale(k):
    if not WIDE:
        return np.ones(k)
    levels = np.array([10, -10, 5, -5, 0])
    a = np.random.permutation(np.resize(levels, k // 512 * 4)).reshape(k // 512, 4)
    idx = np.arange(k)
    return np.exp2(a[idx // 512, idx % 128 // 32])


BF16 = ml_dtypes.bfloat16


def bf(x):
    return np.asarray(x, np.float32).astype(BF16)


def f64(x):
    return np.asarray(x).astype(np.float64)


B, G, D, H, DH, R, F, L = 1, 32, 1024, 4, 512, 200, 4096, 2
S = G * G
INNER = H * DH
ROT = 2 * R
MAX_FREQ = 10.0
EPS = 1e-5


def make_freqs():
    exps = np.linspace(0.0, np.log(MAX_FREQ / 2.0) / np.log(2.0), R // 2)
    base = (2.0 ** exps) * np.pi
    t = np.linspace(-1.0, 1.0, G)
    f = np.repeat(t[:, None] * base[None, :], 2, axis=-1)
    fh = np.broadcast_to(f[:, None, :], (G, G, R))
    fw = np.broadcast_to(f[None, :, :], (G, G, R))
    return np.concatenate([fh, fw], axis=-1)


def rotate_half(u):
    u = u.reshape(u.shape[:-1] + (u.shape[-1] // 2, 2))
    return np.concatenate([-u[..., 1], u[..., 0]], axis=-1)


def apply_rot(t, cosf, sinf):
    tb = t.reshape(B, H, G, G, DH)
    tl, tr = tb[..., :ROT], tb[..., ROT:]
    tl = tl * cosf + rotate_half(tl) * sinf
    return np.concatenate([tl, tr], axis=-1).reshape(B, H, S, DH)


def to_heads(t):
    return t.reshape(B, S, H, DH).transpose(0, 2, 1, 3)


def setup_inputs():
    s = mx_kscale(D)
    return {'x_grid': bf(np.random.standard_normal((B, S, D))),
            'ln_g': bf((1.0 + 0.1 * np.random.standard_normal(D)) * s),
            'ln_b': bf(0.1 * np.random.standard_normal(D) * s),
            'w_qk': bf(np.random.standard_normal((D, 2 * INNER)) * 1.5 / np.sqrt(D) / s[:, None])}


def reference(x_grid, ln_g, ln_b, w_qk):
    x = f64(x_grid)
    mu = np.mean(x, axis=-1, keepdims=True)
    var = np.mean(np.square(x - mu), axis=-1, keepdims=True)
    xn = (x - mu) / np.sqrt(var + EPS) * f64(ln_g) + f64(ln_b)
    qk = mxq(xn, 2, 'e4m3') @ mxq(f64(w_qk), 0, 'e4m3')
    q, k = to_heads(qk[..., :INNER]), to_heads(qk[..., INNER:])
    freqs = make_freqs()
    cosf, sinf = np.cos(freqs)[None, None], np.sin(freqs)[None, None]
    return apply_rot(q, cosf, sinf), apply_rot(k, cosf, sinf)

@@ -1,0 +1,286 @@
+import math
+from contextlib import ExitStack
+
+import concourse.mybir as mybir
+from concourse.masks import make_identity
+
+F32 = mybir.dt.float32
+BF16 = mybir.dt.bfloat16
+I32 = mybir.dt.int32
+U32 = mybir.dt.uint32
+U8 = mybir.dt.uint8
+FP8X4 = mybir.dt.float8_e4m3fn_x4
+ALU = mybir.AluOpType
+ACT = mybir.ActivationFunctionType
+
+P = 128
+GRID = 32
+TOKENS = GRID * GRID
+FEATURES = 1024
+HEADS = 8
+HEADS_PER_OUTPUT = 4
+CHANNELS = 512
+FREQS = 100
+HALF = 2 * FREQS
+ROTATED = 2 * HALF
+MAX_FREQ = 10.0
+EPS = 1e-5
+
+PACK = 4
+K_PASS = P * PACK
+PASSES = FEATURES // K_PASS
+CHUNKS = FEATURES // P
+TILES = TOKENS // P
+GROUP = 4
+GROUPS = TILES // GROUP
+GROUP_TOKENS = GROUP * P
+BN_WIDTH = 512
+
+QUARTERS = 4
+PIECE_CHANNELS = CHANNELS // QUARTERS
+W_PIECES = PASSES * QUARTERS
+W_LEAD = W_PIECES + 2
+W_BUFS = 3
+
+ROUND_MAGIC = 12582912.0
+
+FLOPS = 2 * TOKENS * FEATURES * HEADS * CHANNELS
+
+
+def regroup(copy, grouped, planes):
+    copy(
+        out=grouped.rearrange("p (c i) t -> p c t i", i=4),
+        in_=planes.rearrange("p t (c i) -> p c t i", i=4),
+    )
+
+
+def tile_transformerencoderlayer_pa_kernel(tc, x_grid, ln_g, ln_b, w_qk, out_0, out_1):
+    nc = tc.nc
+    with ExitStack() as ctx:
+        keep = ctx.enter_context(tc.tile_pool(name="keep", bufs=1))
+        small = ctx.enter_context(tc.tile_pool(name="small", bufs=4))
+        hat_pool = ctx.enter_context(tc.tile_pool(name="hat", bufs=2))
+        stage = ctx.enter_context(tc.tile_pool(name="stage", bufs=2))
+        piece_pool = ctx.enter_context(tc.tile_pool(name="piece", bufs=4))
+        w_pool = ctx.enter_context(tc.tile_pool(name="w", bufs=W_BUFS))
+        y_pool = ctx.enter_context(tc.tile_pool(name="y", bufs=5))
+        cross_pool = ctx.enter_context(tc.tile_pool(name="cross", bufs=3))
+        flip_psum = ctx.enter_context(tc.psum_pool(name="flip", bufs=2))
+        acc_psum = ctx.enter_context(tc.psum_pool(name="acc", bufs=6))
+
+        gain_bias_rows = keep.tile([P, P], BF16)
+        nc.vector.memset(gain_bias_rows[:], 0.0)
+        nc.sync.dma_start(out=gain_bias_rows[0:CHUNKS, :], in_=ln_g.rearrange("(c p) -> c p", p=P))
+        nc.sync.dma_start(out=gain_bias_rows[CHUNKS : 2 * CHUNKS, :], in_=ln_b.rearrange("(c p) -> c p", p=P))
+
+        x_sb = keep.tile([P, TILES, FEATURES], BF16)
+        x_view = x_grid[0].rearrange("(p i) d -> p i d", i=TILES)
+
+        def load_x(group):
+            for pair in range(group * GROUP, (group + 1) * GROUP, 2):
+                nc.sync.dma_start(out=x_sb[:, pair : pair + 2, :], in_=x_view[:, pair : pair + 2, :])
+
+        w_view = w_qk.rearrange("(g t p) n -> p g t n", t=PACK, p=P)
+
+        w_raw = {}
+
+        def load_w(head):
+            w_raw[head] = w_pool.tile([P, PASSES, PACK, CHANNELS], BF16, name="w_raw")
+            nc.sync.dma_start(out=w_raw[head][:], in_=w_view[:, :, :, head * CHANNELS : (head + 1) * CHANNELS])
+
+        load_x(0)
+        load_w(0)
+        load_x(1)
+        for head in range(1, W_BUFS):
+            load_w(head)
+
+        token = keep.tile([P, TILES], I32)
+        nc.gpsimd.iota(token[:], pattern=[[1, TILES]], base=0, channel_multiplier=TILES)
+
+        freq = keep.tile([P, P], F32)
+        ratio = (MAX_FREQ / 2.0) ** (1.0 / (FREQS - 1))
+        nc.vector.memset(freq[:, 0:1], 0.5)
+        for doubling in range(7):
+            filled = 2**doubling
+            nc.vector.tensor_scalar_mul(
+                out=freq[:, filled : 2 * filled], in0=freq[:, 0:filled], scalar1=ratio**filled
+            )
+
+        minus_half = keep.tile([P, 1], F32)
+        nc.gpsimd.memset(minus_half[:], -0.5)
+        ident = keep.tile([P, P], F32)
+        make_identity(nc, ident[:])
+
+        gain_bias_f32 = keep.tile([P, P], F32)
+        nc.vector.tensor_copy(out=gain_bias_f32[:], in_=gain_bias_rows[:])
+        gain_bias_ps = flip_psum.tile([P, P], F32, tag="flipped")
+        nc.tensor.transpose(gain_bias_ps[:], gain_bias_f32[:], ident[:])
+        gain_bias = keep.tile([P, 2 * CHUNKS], F32)
+        nc.vector.tensor_copy(out=gain_bias[:], in_=gain_bias_ps[:, 0 : 2 * CHUNKS])
+
+        xn_t = keep.tile([P, CHUNKS, TOKENS], BF16)
+        x_codes = keep.tile([P, PASSES, TOKENS], U32, align_bytes=64)
+        x_scales = keep.tile([P, PASSES, TOKENS], U8, align_bytes=64)
+
+        def layer_norm_group(group):
+            group_cols = slice(group * GROUP_TOKENS, (group + 1) * GROUP_TOKENS)
+            x_hat = hat_pool.tile([P, GROUP, FEATURES], F32)
+            for a in range(GROUP):
+                x_tile = x_sb[:, group * GROUP + a, :]
+                stats = small.tile([P, FEATURES // BN_WIDTH, 6], F32)
+                for part in range(FEATURES // BN_WIDTH):
+                    nc.vector.bn_stats(out=stats[:, part, :], in_=x_tile[:, part * BN_WIDTH : (part + 1) * BN_WIDTH])
+                mean_var = small.tile([P, 2], F32)
+                nc.vector.bn_aggr(out=mean_var[:], in_=stats[:].rearrange("p a s -> p (a s)"))
+                neg_mean = small.tile([P, 1], F32)
+                nc.vector.tensor_scalar_mul(out=neg_mean[:], in0=mean_var[:, 0:1], scalar1=-1.0)
+                var_eps = small.tile([P, 1], F32)
+                nc.vector.tensor_scalar_add(out=var_eps[:], in0=mean_var[:, 1:2], scalar1=EPS)
+                rstd = small.tile([P, 1], F32)
+                nc.gpsimd.tensor_tensor(out=rstd[:], in0=var_eps[:], in1=minus_half[:], op=ALU.pow)
+                nc.gpsimd.tensor_scalar(
+                    out=x_hat[:, a, :], in0=x_tile, scalar1=neg_mean[:], scalar2=rstd[:], op0=ALU.add, op1=ALU.mult
+                )
+
+            for c in range(CHUNKS):
+                flipped = flip_psum.tile([P, GROUP, P], F32, tag="flipped")
+                for a in range(GROUP):
+                    nc.tensor.transpose(flipped[:, a, :], x_hat[:, a, c * P : (c + 1) * P], ident[:])
+                nc.scalar.activation(
+                    out=xn_t[:, c, group_cols],
+                    in_=flipped[:].rearrange("p a m -> p (a m)"),
+                    func=ACT.Identity,
+                    scale=gain_bias[:, c : c + 1],
+                    bias=gain_bias[:, CHUNKS + c : CHUNKS + c + 1],
+                )
+
+            for g in range(PASSES):
+                xn_grouped = stage.tile([P, GROUP_TOKENS, PACK], BF16, align_bytes=64)
+                regroup(nc.vector.tensor_copy, xn_grouped[:], xn_t[:, g * PACK : (g + 1) * PACK, group_cols])
+                nc.vector.quantize_mx(
+                    out=x_codes[:, g, group_cols].bitcast(FP8X4),
+                    scales=x_scales[:, g, group_cols],
+                    in_=xn_grouped[:].rearrange("p c t -> p (c t)"),
+                )
+
+        w_codes = {}
+        w_scales = {}
+
+        def prepare_w_piece(number):
+            head, piece = divmod(number, W_PIECES)
+            g, quarter = divmod(piece, QUARTERS)
+            piece_cols = slice(quarter * PIECE_CHANNELS, (quarter + 1) * PIECE_CHANNELS)
+            if piece == 0:
+                w_codes[head] = w_pool.tile([P, PASSES, CHANNELS], U32, align_bytes=64, name="w_codes")
+                w_scales[head] = w_pool.tile([P, PASSES, CHANNELS], U8, align_bytes=64, name="w_scales")
+            w_grouped = piece_pool.tile([P, PIECE_CHANNELS, PACK], BF16, align_bytes=64)
+            regroup(nc.scalar.copy, w_grouped[:], w_raw[head][:, g, :, piece_cols])
+            nc.vector.quantize_mx(
+                out=w_codes[head][:, g, piece_cols].bitcast(FP8X4),
+                scales=w_scales[head][:, g, piece_cols],
+                in_=w_grouped[:].rearrange("p c t -> p (c t)"),
+            )
+            if piece == W_PIECES - 1 and head + W_BUFS < HEADS:
+                load_w(head + W_BUFS)
+
+        layer_norm_group(0)
+        for number in range(W_LEAD):
+            prepare_w_piece(number)
+
+        blocks = TILES + 1
+        grid_index = keep.tile([P, blocks], I32)
+        nc.vector.tensor_single_scalar(out=grid_index[:, 0:TILES], in_=token[:], scalar=GRID - 1, op=ALU.bitwise_and)
+        nc.vector.tensor_single_scalar(
+            out=grid_index[:, TILES:blocks], in_=token[:, 0:1], scalar=5, op=ALU.arith_shift_right
+        )
+        coord = keep.tile([P, blocks], F32)
+        nc.vector.tensor_scalar(
+            out=coord[:], in0=grid_index[:], scalar1=2.0 / (GRID - 1), scalar2=-1.0, op0=ALU.mult, op1=ALU.add
+        )
+        turn = keep.tile([P, blocks, FREQS], F32)
+        nc.vector.tensor_tensor(
+            out=turn[:],
+            in0=freq[:, 0:FREQS].unsqueeze(1).to_broadcast([P, blocks, FREQS]),
+            in1=coord[:].unsqueeze(2).to_broadcast([P, blocks, FREQS]),
+            op=ALU.mult,
+        )
+        rounded = keep.tile([P, blocks, FREQS], F32)
+        nc.vector.tensor_scalar_add(out=rounded[:], in0=turn[:], scalar1=ROUND_MAGIC)
+        back = keep.tile([P, blocks, FREQS], F32)
+        nc.vector.scalar_tensor_tensor(
+            out=back[:].rearrange("p b j -> p (b j)"),
+            in0=rounded[:].rearrange("p b j -> p (b j)"),
+            scalar=ROUND_MAGIC,
+            in1=turn[:].rearrange("p b j -> p (b j)"),
+            op0=ALU.subtract,
+            op1=ALU.subtract,
+        )
+        dist = keep.tile([P, blocks, FREQS], F32)
+        nc.vector.scalar_tensor_tensor(
+            out=dist[:].rearrange("p b j -> p (b j)"),
+            in0=back[:].rearrange("p b j -> p (b j)"),
+            scalar=-1.0,
+            in1=back[:].rearrange("p b j -> p (b j)"),
+            op0=ALU.mult,
+            op1=ALU.max,
+        )
+        two_pi = 2.0 * math.pi
+        cos_tab = keep.tile([P, blocks, FREQS], F32)
+        sin_tab = keep.tile([P, blocks, FREQS], F32)
+        nc.scalar.activation(
+            out=cos_tab[:, 1:blocks, :], in_=dist[:, 0:TILES, :], func=ACT.Sin, scale=-two_pi, bias=math.pi / 2.0
+        )
+        nc.scalar.activation(
+            out=cos_tab[:, 0:1, :], in_=dist[:, TILES:blocks, :], func=ACT.Sin, scale=-two_pi, bias=math.pi / 2.0
+        )
+        nc.scalar.activation(out=sin_tab[:, 0:TILES, :], in_=back[:, 0:TILES, :], func=ACT.Sin, scale=-two_pi)
+        nc.scalar.activation(out=sin_tab[:, TILES:blocks, :], in_=back[:, TILES:blocks, :], func=ACT.Sin, scale=two_pi)
+
+        layer_norm_group(1)
+
+        for head in range(HEADS):
+            out_tensor = out_0 if head < HEADS_PER_OUTPUT else out_1
+            out_head = out_tensor[0, head % HEADS_PER_OUTPUT].rearrange("(p i) c -> p i c", i=TILES)
+
+            for group in range(GROUPS):
+                y = y_pool.tile([P, GROUP, CHANNELS], F32)
+                cross = cross_pool.tile([P, GROUP, ROTATED], F32)
+                for a in range(GROUP):
+                    i = group * GROUP + a
+                    tile_cols = slice(i * P, (i + 1) * P)
+                    u = acc_psum.tile([P, CHANNELS], F32)
+                    for g in range(PASSES):
+                        nc.tensor.matmul_mx(
+                            out=u[:],
+                            lhsT=x_codes[:, g, tile_cols].bitcast(FP8X4),
+                            lhsT_scale=x_scales[:, g, tile_cols],
+                            rhs=w_codes[head][:, g, :].bitcast(FP8X4),
+                            rhs_scale=w_scales[head][:, g, :],
+                            start=(g == 0),
+                            stop=(g == PASSES - 1),
+                        )
+                    nc.vector.tensor_tensor(
+                        out=y[:, a, 0:ROTATED].rearrange("p (b j d) -> p b j d", b=2, d=2),
+                        in0=u[:, 0:ROTATED].rearrange("p (b j d) -> p b j d", b=2, d=2),
+                        in1=cos_tab[:, 0 : i + 2 : i + 1, :].unsqueeze(3).to_broadcast([P, 2, FREQS, 2]),
+                        op=ALU.mult,
+                    )
+                    nc.vector.tensor_tensor(
+                        out=cross[:, a, :].rearrange("p (e j d) -> p e j d", e=2, d=2),
+                        in0=u[:, 0:ROTATED].rearrange("p (j d e) -> p e j d", d=2, e=2),
+                        in1=sin_tab[:, i : blocks : TILES - i, :].unsqueeze(3).to_broadcast([P, 2, FREQS, 2]),
+                        op=ALU.mult,
+                    )
+                    nc.scalar.copy(out=y[:, a, ROTATED:CHANNELS], in_=u[:, ROTATED:CHANNELS])
+
+                    number = head * TILES + i + W_LEAD
+                    if number < HEADS * W_PIECES:
+                        prepare_w_piece(number)
+
+                nc.gpsimd.tensor_tensor(
+                    out=y[:, :, 0:HALF], in0=y[:, :, 0:HALF], in1=cross[:, :, HALF:ROTATED], op=ALU.add
+                )
+                nc.gpsimd.tensor_tensor(
+                    out=y[:, :, HALF:ROTATED], in0=y[:, :, HALF:ROTATED], in1=cross[:, :, 0:HALF], op=ALU.add
+                )
+                nc.sync.dma_start(out=out_head[:, group * GROUP : (group + 1) * GROUP, :], in_=y[:])

@@ -261,14 +261,14 @@ def tile_transformerencoderlayer_pa_kernel(tc, x_grid, ln_g, ln_b, w_qk, out_0, 
                         )
                     nc.vector.tensor_tensor(
                         out=y[:, a, 0:ROTATED].rearrange("p (b j d) -> p b j d", b=2, d=2),
-                        in0=u[:, 0:ROTATED].rearrange("p (b j d) -> p b j d", b=2, d=2),
-                        in1=cos_tab[:, 0 : i + 2 : i + 1, :].unsqueeze(3).to_broadcast([P, 2, FREQS, 2]),
+                        in0=cos_tab[:, 0 : i + 2 : i + 1, :].unsqueeze(3).to_broadcast([P, 2, FREQS, 2]),
+                        in1=u[:, 0:ROTATED].rearrange("p (b j d) -> p b j d", b=2, d=2),
                         op=ALU.mult,
                     )
                     nc.vector.tensor_tensor(
                         out=cross[:, a, :].rearrange("p (e j d) -> p e j d", e=2, d=2),
-                        in0=u[:, 0:ROTATED].rearrange("p (j d e) -> p e j d", d=2, e=2),
-                        in1=sin_tab[:, i : blocks : TILES - i, :].unsqueeze(3).to_broadcast([P, 2, FREQS, 2]),
+                        in0=sin_tab[:, i : blocks : TILES - i, :].unsqueeze(3).to_broadcast([P, 2, FREQS, 2]),
+                        in1=u[:, 0:ROTATED].rearrange("p (j d e) -> p e j d", d=2, e=2),
                         op=ALU.mult,
                     )
                     nc.scalar.copy(out=y[:, a, ROTATED:CHANNELS], in_=u[:, ROTATED:CHANNELS])

@@ -261,14 +261,14 @@ def tile_transformerencoderlayer_pa_kernel(tc, x_grid, ln_g, ln_b, w_qk, out_0, 
                         )
                     nc.vector.tensor_tensor(
                         out=y[:, a, 0:ROTATED].rearrange("p (b j d) -> p b j d", b=2, d=2),
-                        in0=cos_tab[:, 0 : i + 2 : i + 1, :].unsqueeze(3).to_broadcast([P, 2, FREQS, 2]),
-                        in1=u[:, 0:ROTATED].rearrange("p (b j d) -> p b j d", b=2, d=2),
+                        in0=u[:, 0:ROTATED].rearrange("p (b j d) -> p b j d", b=2, d=2),
+                        in1=cos_tab[:, 0 : i + 2 : i + 1, :].unsqueeze(3).to_broadcast([P, 2, FREQS, 2]),
                         op=ALU.mult,
                     )
                     nc.vector.tensor_tensor(
                         out=cross[:, a, :].rearrange("p (e j d) -> p e j d", e=2, d=2),
-                        in0=sin_tab[:, i : blocks : TILES - i, :].unsqueeze(3).to_broadcast([P, 2, FREQS, 2]),
-                        in1=u[:, 0:ROTATED].rearrange("p (j d e) -> p e j d", d=2, e=2),
+                        in0=u[:, 0:ROTATED].rearrange("p (j d e) -> p e j d", d=2, e=2),
+                        in1=sin_tab[:, i : blocks : TILES - i, :].unsqueeze(3).to_broadcast([P, 2, FREQS, 2]),
                         op=ALU.mult,
                     )
                     nc.scalar.copy(out=y[:, a, ROTATED:CHANNELS], in_=u[:, ROTATED:CHANNELS])
@@ -277,10 +277,10 @@ def tile_transformerencoderlayer_pa_kernel(tc, x_grid, ln_g, ln_b, w_qk, out_0, 
                     if number < HEADS * W_PIECES:
                         prepare_w_piece(number)
 
-                nc.gpsimd.tensor_tensor(
+                nc.vector.tensor_tensor(
                     out=y[:, :, 0:HALF], in0=y[:, :, 0:HALF], in1=cross[:, :, HALF:ROTATED], op=ALU.add
                 )
-                nc.gpsimd.tensor_tensor(
+                nc.vector.tensor_tensor(
                     out=y[:, :, HALF:ROTATED], in0=y[:, :, HALF:ROTATED], in1=cross[:, :, 0:HALF], op=ALU.add
                 )
                 nc.sync.dma_start(out=out_head[:, group * GROUP : (group + 1) * GROUP, :], in_=y[:])

@@ -61,7 +61,7 @@ def tile_transformerencoderlayer_pa_kernel(tc, x_grid, ln_g, ln_b, w_qk, out_0, 
         small = ctx.enter_context(tc.tile_pool(name="small", bufs=4))
         hat_pool = ctx.enter_context(tc.tile_pool(name="hat", bufs=2))
         stage = ctx.enter_context(tc.tile_pool(name="stage", bufs=2))
-        piece_pool = ctx.enter_context(tc.tile_pool(name="piece", bufs=4))
+        grouped_pool = ctx.enter_context(tc.tile_pool(name="grouped", bufs=2))
         w_pool = ctx.enter_context(tc.tile_pool(name="w", bufs=W_BUFS))
         y_pool = ctx.enter_context(tc.tile_pool(name="y", bufs=5))
         cross_pool = ctx.enter_context(tc.tile_pool(name="cross", bufs=3))
@@ -163,6 +163,7 @@ def tile_transformerencoderlayer_pa_kernel(tc, x_grid, ln_g, ln_b, w_qk, out_0, 
                     in_=xn_grouped[:].rearrange("p c t -> p (c t)"),
                 )
 
+        w_grouped = {}
         w_codes = {}
         w_scales = {}
 
@@ -171,17 +172,20 @@ def tile_transformerencoderlayer_pa_kernel(tc, x_grid, ln_g, ln_b, w_qk, out_0, 
             g, quarter = divmod(piece, QUARTERS)
             piece_cols = slice(quarter * PIECE_CHANNELS, (quarter + 1) * PIECE_CHANNELS)
             if piece == 0:
+                w_grouped[head] = grouped_pool.tile(
+                    [P, PASSES, CHANNELS, PACK], BF16, align_bytes=64, name="w_grouped"
+                )
+            regroup(nc.scalar.copy, w_grouped[head][:, g, piece_cols, :], w_raw[head][:, g, :, piece_cols])
+            if piece == W_PIECES - 1:
                 w_codes[head] = w_pool.tile([P, PASSES, CHANNELS], U32, align_bytes=64, name="w_codes")
                 w_scales[head] = w_pool.tile([P, PASSES, CHANNELS], U8, align_bytes=64, name="w_scales")
-            w_grouped = piece_pool.tile([P, PIECE_CHANNELS, PACK], BF16, align_bytes=64)
-            regroup(nc.scalar.copy, w_grouped[:], w_raw[head][:, g, :, piece_cols])
-            nc.vector.quantize_mx(
-                out=w_codes[head][:, g, piece_cols].bitcast(FP8X4),
-                scales=w_scales[head][:, g, piece_cols],
-                in_=w_grouped[:].rearrange("p c t -> p (c t)"),
-            )
-            if piece == W_PIECES - 1 and head + W_BUFS < HEADS:
-                load_w(head + W_BUFS)
+                nc.vector.quantize_mx(
+                    out=w_codes[head][:].rearrange("p g c -> p (g c)").bitcast(FP8X4),
+                    scales=w_scales[head][:].rearrange("p g c -> p (g c)"),
+                    in_=w_grouped[head][:].rearrange("p g c t -> p (g c t)"),
+                )
+                if head + W_BUFS < HEADS:
+                    load_w(head + W_BUFS)
 
         layer_norm_group(0)
         for number in range(W_LEAD):
@@ -277,10 +281,10 @@ def tile_transformerencoderlayer_pa_kernel(tc, x_grid, ln_g, ln_b, w_qk, out_0, 
                     if number < HEADS * W_PIECES:
                         prepare_w_piece(number)
 
-                nc.vector.tensor_tensor(
+                nc.gpsimd.tensor_tensor(
                     out=y[:, :, 0:HALF], in0=y[:, :, 0:HALF], in1=cross[:, :, HALF:ROTATED], op=ALU.add
                 )
-                nc.vector.tensor_tensor(
+                nc.gpsimd.tensor_tensor(
                     out=y[:, :, HALF:ROTATED], in0=y[:, :, HALF:ROTATED], in1=cross[:, :, 0:HALF], op=ALU.add
                 )
                 nc.sync.dma_start(out=out_head[:, group * GROUP : (group + 1) * GROUP, :], in_=y[:])

@@ -33,7 +33,9 @@ CHUNKS = FEATURES // P
 TILES = TOKENS // P
 GROUP = 4
 GROUPS = TILES // GROUP
-GROUP_TOKENS = GROUP * P
+LN_GROUP = 2
+LN_GROUPS = TILES // LN_GROUP
+LN_TOKENS = LN_GROUP * P
 BN_WIDTH = 512
 
 QUARTERS = 4
@@ -58,15 +60,14 @@ def tile_transformerencoderlayer_pa_kernel(tc, x_grid, ln_g, ln_b, w_qk, out_0, 
     nc = tc.nc
     with ExitStack() as ctx:
         keep = ctx.enter_context(tc.tile_pool(name="keep", bufs=1))
-        small = ctx.enter_context(tc.tile_pool(name="small", bufs=4))
-        hat_pool = ctx.enter_context(tc.tile_pool(name="hat", bufs=2))
+        small = ctx.enter_context(tc.tile_pool(name="small", bufs=TILES))
+        hat_pool = ctx.enter_context(tc.tile_pool(name="hat", bufs=LN_GROUPS))
         stage = ctx.enter_context(tc.tile_pool(name="stage", bufs=2))
         grouped_pool = ctx.enter_context(tc.tile_pool(name="grouped", bufs=2))
         w_pool = ctx.enter_context(tc.tile_pool(name="w", bufs=W_BUFS))
         y_pool = ctx.enter_context(tc.tile_pool(name="y", bufs=5))
         cross_pool = ctx.enter_context(tc.tile_pool(name="cross", bufs=3))
-        flip_psum = ctx.enter_context(tc.psum_pool(name="flip", bufs=2))
-        acc_psum = ctx.enter_context(tc.psum_pool(name="acc", bufs=6))
+        psum = ctx.enter_context(tc.psum_pool(name="psum", bufs=8))
 
         gain_bias_rows = keep.tile([P, P], BF16)
         nc.vector.memset(gain_bias_rows[:], 0.0)
@@ -81,7 +82,6 @@ def tile_transformerencoderlayer_pa_kernel(tc, x_grid, ln_g, ln_b, w_qk, out_0, 
                 nc.sync.dma_start(out=x_sb[:, pair : pair + 2, :], in_=x_view[:, pair : pair + 2, :])
 
         w_view = w_qk.rearrange("(g t p) n -> p g t n", t=PACK, p=P)
-
         w_raw = {}
 
         def load_w(head):
@@ -96,6 +96,10 @@ def tile_transformerencoderlayer_pa_kernel(tc, x_grid, ln_g, ln_b, w_qk, out_0, 
 
         token = keep.tile([P, TILES], I32)
         nc.gpsimd.iota(token[:], pattern=[[1, TILES]], base=0, channel_multiplier=TILES)
+        minus_half = keep.tile([P, 1], F32)
+        nc.gpsimd.memset(minus_half[:], -0.5)
+        ident = keep.tile([P, P], F32)
+        make_identity(nc, ident[:])
 
         freq = keep.tile([P, P], F32)
         ratio = (MAX_FREQ / 2.0) ** (1.0 / (FREQS - 1))
@@ -105,92 +109,6 @@ def tile_transformerencoderlayer_pa_kernel(tc, x_grid, ln_g, ln_b, w_qk, out_0, 
             nc.vector.tensor_scalar_mul(
                 out=freq[:, filled : 2 * filled], in0=freq[:, 0:filled], scalar1=ratio**filled
             )
-
-        minus_half = keep.tile([P, 1], F32)
-        nc.gpsimd.memset(minus_half[:], -0.5)
-        ident = keep.tile([P, P], F32)
-        make_identity(nc, ident[:])
-
-        gain_bias_f32 = keep.tile([P, P], F32)
-        nc.vector.tensor_copy(out=gain_bias_f32[:], in_=gain_bias_rows[:])
-        gain_bias_ps = flip_psum.tile([P, P], F32, tag="flipped")
-        nc.tensor.transpose(gain_bias_ps[:], gain_bias_f32[:], ident[:])
-        gain_bias = keep.tile([P, 2 * CHUNKS], F32)
-        nc.vector.tensor_copy(out=gain_bias[:], in_=gain_bias_ps[:, 0 : 2 * CHUNKS])
-
-        xn_t = keep.tile([P, CHUNKS, TOKENS], BF16)
-        x_codes = keep.tile([P, PASSES, TOKENS], U32, align_bytes=64)
-        x_scales = keep.tile([P, PASSES, TOKENS], U8, align_bytes=64)
-
-        def layer_norm_group(group):
-            group_cols = slice(group * GROUP_TOKENS, (group + 1) * GROUP_TOKENS)
-            x_hat = hat_pool.tile([P, GROUP, FEATURES], F32)
-            for a in range(GROUP):
-                x_tile = x_sb[:, group * GROUP + a, :]
-                stats = small.tile([P, FEATURES // BN_WIDTH, 6], F32)
-                for part in range(FEATURES // BN_WIDTH):
-                    nc.vector.bn_stats(out=stats[:, part, :], in_=x_tile[:, part * BN_WIDTH : (part + 1) * BN_WIDTH])
-                mean_var = small.tile([P, 2], F32)
-                nc.vector.bn_aggr(out=mean_var[:], in_=stats[:].rearrange("p a s -> p (a s)"))
-                neg_mean = small.tile([P, 1], F32)
-                nc.vector.tensor_scalar_mul(out=neg_mean[:], in0=mean_var[:, 0:1], scalar1=-1.0)
-                var_eps = small.tile([P, 1], F32)
-                nc.vector.tensor_scalar_add(out=var_eps[:], in0=mean_var[:, 1:2], scalar1=EPS)
-                rstd = small.tile([P, 1], F32)
-                nc.gpsimd.tensor_tensor(out=rstd[:], in0=var_eps[:], in1=minus_half[:], op=ALU.pow)
-                nc.gpsimd.tensor_scalar(
-                    out=x_hat[:, a, :], in0=x_tile, scalar1=neg_mean[:], scalar2=rstd[:], op0=ALU.add, op1=ALU.mult
-                )
-
-            for c in range(CHUNKS):
-                flipped = flip_psum.tile([P, GROUP, P], F32, tag="flipped")
-                for a in range(GROUP):
-                    nc.tensor.transpose(flipped[:, a, :], x_hat[:, a, c * P : (c + 1) * P], ident[:])
-                nc.scalar.activation(
-                    out=xn_t[:, c, group_cols],
-                    in_=flipped[:].rearrange("p a m -> p (a m)"),
-                    func=ACT.Identity,
-                    scale=gain_bias[:, c : c + 1],
-                    bias=gain_bias[:, CHUNKS + c : CHUNKS + c + 1],
-                )
-
-            for g in range(PASSES):
-                xn_grouped = stage.tile([P, GROUP_TOKENS, PACK], BF16, align_bytes=64)
-                regroup(nc.vector.tensor_copy, xn_grouped[:], xn_t[:, g * PACK : (g + 1) * PACK, group_cols])
-                nc.vector.quantize_mx(
-                    out=x_codes[:, g, group_cols].bitcast(FP8X4),
-                    scales=x_scales[:, g, group_cols],
-                    in_=xn_grouped[:].rearrange("p c t -> p (c t)"),
-                )
-
-        w_grouped = {}
-        w_codes = {}
-        w_scales = {}
-
-        def prepare_w_piece(number):
-            head, piece = divmod(number, W_PIECES)
-            g, quarter = divmod(piece, QUARTERS)
-            piece_cols = slice(quarter * PIECE_CHANNELS, (quarter + 1) * PIECE_CHANNELS)
-            if piece == 0:
-                w_grouped[head] = grouped_pool.tile(
-                    [P, PASSES, CHANNELS, PACK], BF16, align_bytes=64, name="w_grouped"
-                )
-            regroup(nc.scalar.copy, w_grouped[head][:, g, piece_cols, :], w_raw[head][:, g, :, piece_cols])
-            if piece == W_PIECES - 1:
-                w_codes[head] = w_pool.tile([P, PASSES, CHANNELS], U32, align_bytes=64, name="w_codes")
-                w_scales[head] = w_pool.tile([P, PASSES, CHANNELS], U8, align_bytes=64, name="w_scales")
-                nc.vector.quantize_mx(
-                    out=w_codes[head][:].rearrange("p g c -> p (g c)").bitcast(FP8X4),
-                    scales=w_scales[head][:].rearrange("p g c -> p (g c)"),
-                    in_=w_grouped[head][:].rearrange("p g c t -> p (g c t)"),
-                )
-                if head + W_BUFS < HEADS:
-                    load_w(head + W_BUFS)
-
-        layer_norm_group(0)
-        for number in range(W_LEAD):
-            prepare_w_piece(number)
-
         blocks = TILES + 1
         grid_index = keep.tile([P, blocks], I32)
         nc.vector.tensor_single_scalar(out=grid_index[:, 0:TILES], in_=token[:], scalar=GRID - 1, op=ALU.bitwise_and)
@@ -229,62 +147,163 @@ def tile_transformerencoderlayer_pa_kernel(tc, x_grid, ln_g, ln_b, w_qk, out_0, 
             op1=ALU.max,
         )
         two_pi = 2.0 * math.pi
-        cos_tab = keep.tile([P, blocks, FREQS], F32)
         sin_tab = keep.tile([P, blocks, FREQS], F32)
+        cos_tab = keep.tile([P, blocks, FREQS], F32)
+        nc.scalar.activation(out=sin_tab[:, 0:TILES, :], in_=back[:, 0:TILES, :], func=ACT.Sin, scale=-two_pi)
+        nc.scalar.activation(out=sin_tab[:, TILES:blocks, :], in_=back[:, TILES:blocks, :], func=ACT.Sin, scale=two_pi)
         nc.scalar.activation(
             out=cos_tab[:, 1:blocks, :], in_=dist[:, 0:TILES, :], func=ACT.Sin, scale=-two_pi, bias=math.pi / 2.0
         )
         nc.scalar.activation(
             out=cos_tab[:, 0:1, :], in_=dist[:, TILES:blocks, :], func=ACT.Sin, scale=-two_pi, bias=math.pi / 2.0
         )
-        nc.scalar.activation(out=sin_tab[:, 0:TILES, :], in_=back[:, 0:TILES, :], func=ACT.Sin, scale=-two_pi)
-        nc.scalar.activation(out=sin_tab[:, TILES:blocks, :], in_=back[:, TILES:blocks, :], func=ACT.Sin, scale=two_pi)
 
-        layer_norm_group(1)
+        gain_bias_f32 = keep.tile([P, P], F32)
+        nc.vector.tensor_copy(out=gain_bias_f32[:], in_=gain_bias_rows[:])
+        gain_bias_ps = psum.tile([P, P], F32, tag="bank")
+        nc.tensor.transpose(gain_bias_ps[:], gain_bias_f32[:], ident[:])
+        gain_bias = keep.tile([P, 2 * CHUNKS], F32)
 
-        for head in range(HEADS):
+        x_hat = {}
+        xn_t = keep.tile([P, CHUNKS, TOKENS], BF16)
+        x_codes = keep.tile([P, PASSES, TOKENS], U32, align_bytes=64)
+        x_scales = keep.tile([P, PASSES, TOKENS], U8, align_bytes=64)
+
+        def normalise(i):
+            group, a = divmod(i, LN_GROUP)
+            if a == 0:
+                x_hat[group] = hat_pool.tile([P, LN_GROUP, FEATURES], F32, name="x_hat")
+            x_tile = x_sb[:, i, :]
+            stats = small.tile([P, FEATURES // BN_WIDTH, 6], F32)
+            for part in range(FEATURES // BN_WIDTH):
+                nc.vector.bn_stats(out=stats[:, part, :], in_=x_tile[:, part * BN_WIDTH : (part + 1) * BN_WIDTH])
+            mean_var = small.tile([P, 2], F32)
+            nc.vector.bn_aggr(out=mean_var[:], in_=stats[:].rearrange("p a s -> p (a s)"))
+            neg_mean = small.tile([P, 1], F32)
+            nc.vector.tensor_scalar_mul(out=neg_mean[:], in0=mean_var[:, 0:1], scalar1=-1.0)
+            var_eps = small.tile([P, 1], F32)
+            nc.vector.tensor_scalar_add(out=var_eps[:], in0=mean_var[:, 1:2], scalar1=EPS)
+            rstd = small.tile([P, 1], F32)
+            nc.gpsimd.tensor_tensor(out=rstd[:], in0=var_eps[:], in1=minus_half[:], op=ALU.pow)
+            nc.gpsimd.tensor_scalar(
+                out=x_hat[group][:, a, :], in0=x_tile, scalar1=neg_mean[:], scalar2=rstd[:], op0=ALU.add, op1=ALU.mult
+            )
+
+        def flip(group, c):
+            flipped = psum.tile([P, LN_GROUP, P], F32, tag="bank")
+            for a in range(LN_GROUP):
+                nc.tensor.transpose(flipped[:, a, :], x_hat[group][:, a, c * P : (c + 1) * P], ident[:])
+            nc.scalar.activation(
+                out=xn_t[:, c, group * LN_TOKENS : (group + 1) * LN_TOKENS],
+                in_=flipped[:].rearrange("p a m -> p (a m)"),
+                func=ACT.Identity,
+                scale=gain_bias[:, c : c + 1],
+                bias=gain_bias[:, CHUNKS + c : CHUNKS + c + 1],
+            )
+
+        def quantise_x(group, g):
+            group_cols = slice(group * LN_TOKENS, (group + 1) * LN_TOKENS)
+            xn_grouped = stage.tile([P, LN_TOKENS, PACK], BF16, align_bytes=64)
+            regroup(nc.vector.tensor_copy, xn_grouped[:], xn_t[:, g * PACK : (g + 1) * PACK, group_cols])
+            nc.vector.quantize_mx(
+                out=x_codes[:, g, group_cols].bitcast(FP8X4),
+                scales=x_scales[:, g, group_cols],
+                in_=xn_grouped[:].rearrange("p c t -> p (c t)"),
+            )
+
+        w_grouped = {}
+        w_codes = {}
+        w_scales = {}
+
+        def regroup_w_piece(number):
+            head, piece = divmod(number, W_PIECES)
+            g, quarter = divmod(piece, QUARTERS)
+            piece_cols = slice(quarter * PIECE_CHANNELS, (quarter + 1) * PIECE_CHANNELS)
+            if piece == 0:
+                w_grouped[head] = grouped_pool.tile(
+                    [P, PASSES, CHANNELS, PACK], BF16, align_bytes=64, name="w_grouped"
+                )
+            regroup(nc.scalar.copy, w_grouped[head][:, g, piece_cols, :], w_raw[head][:, g, :, piece_cols])
+            if piece == W_PIECES - 1 and head + W_BUFS < HEADS:
+                load_w(head + W_BUFS)
+
+        def quantise_w(head):
+            w_codes[head] = w_pool.tile([P, PASSES, CHANNELS], U32, align_bytes=64, name="w_codes")
+            w_scales[head] = w_pool.tile([P, PASSES, CHANNELS], U8, align_bytes=64, name="w_scales")
+            nc.vector.quantize_mx(
+                out=w_codes[head][:].rearrange("p g c -> p (g c)").bitcast(FP8X4),
+                scales=w_scales[head][:].rearrange("p g c -> p (g c)"),
+                in_=w_grouped[head][:].rearrange("p g c t -> p (g c t)"),
+            )
+
+        u_banks = {}
+
+        def project_group(head, group):
+            for i in range(group * GROUP, (group + 1) * GROUP):
+                tile_cols = slice(i * P, (i + 1) * P)
+                u_banks[(head, i)] = psum.tile([P, CHANNELS], F32, tag="bank", name="u")
+                for g in range(PASSES):
+                    nc.tensor.matmul_mx(
+                        out=u_banks[(head, i)][:],
+                        lhsT=x_codes[:, g, tile_cols].bitcast(FP8X4),
+                        lhsT_scale=x_scales[:, g, tile_cols],
+                        rhs=w_codes[head][:, g, :].bitcast(FP8X4),
+                        rhs_scale=w_scales[head][:, g, :],
+                        start=(g == 0),
+                        stop=(g == PASSES - 1),
+                    )
+
+        def rotate_group(head, group):
+            y = y_pool.tile([P, GROUP, CHANNELS], F32)
+            cross = cross_pool.tile([P, GROUP, ROTATED], F32)
+            for a in range(GROUP):
+                i = group * GROUP + a
+                u = u_banks[(head, i)]
+                step = head * TILES + i
+                if step + W_LEAD < HEADS * W_PIECES:
+                    regroup_w_piece(step + W_LEAD)
+                nc.vector.tensor_tensor(
+                    out=y[:, a, 0:ROTATED].rearrange("p (b j d) -> p b j d", b=2, d=2),
+                    in0=u[:, 0:ROTATED].rearrange("p (b j d) -> p b j d", b=2, d=2),
+                    in1=cos_tab[:, 0 : i + 2 : i + 1, :].unsqueeze(3).to_broadcast([P, 2, FREQS, 2]),
+                    op=ALU.mult,
+                )
+                nc.vector.tensor_tensor(
+                    out=cross[:, a, :].rearrange("p (e j d) -> p e j d", e=2, d=2),
+                    in0=u[:, 0:ROTATED].rearrange("p (j d e) -> p e j d", d=2, e=2),
+                    in1=sin_tab[:, i : blocks : TILES - i, :].unsqueeze(3).to_broadcast([P, 2, FREQS, 2]),
+                    op=ALU.mult,
+                )
+                nc.scalar.copy(out=y[:, a, ROTATED:CHANNELS], in_=u[:, ROTATED:CHANNELS])
+                if (step + W_LEAD) % W_PIECES == 0 and step + W_LEAD <= HEADS * W_PIECES:
+                    quantise_w((step + W_LEAD) // W_PIECES - 1)
+
+            last = head == HEADS - 1 and group == GROUPS - 1
+            adder = nc.vector if last else nc.gpsimd
+            adder.tensor_tensor(out=y[:, :, 0:HALF], in0=y[:, :, 0:HALF], in1=cross[:, :, HALF:ROTATED], op=ALU.add)
+            adder.tensor_tensor(
+                out=y[:, :, HALF:ROTATED], in0=y[:, :, HALF:ROTATED], in1=cross[:, :, 0:HALF], op=ALU.add
+            )
             out_tensor = out_0 if head < HEADS_PER_OUTPUT else out_1
             out_head = out_tensor[0, head % HEADS_PER_OUTPUT].rearrange("(p i) c -> p i c", i=TILES)
+            nc.sync.dma_start(out=out_head[:, group * GROUP : (group + 1) * GROUP, :], in_=y[:])
 
-            for group in range(GROUPS):
-                y = y_pool.tile([P, GROUP, CHANNELS], F32)
-                cross = cross_pool.tile([P, GROUP, ROTATED], F32)
-                for a in range(GROUP):
-                    i = group * GROUP + a
-                    tile_cols = slice(i * P, (i + 1) * P)
-                    u = acc_psum.tile([P, CHANNELS], F32)
-                    for g in range(PASSES):
-                        nc.tensor.matmul_mx(
-                            out=u[:],
-                            lhsT=x_codes[:, g, tile_cols].bitcast(FP8X4),
-                            lhsT_scale=x_scales[:, g, tile_cols],
-                            rhs=w_codes[head][:, g, :].bitcast(FP8X4),
-                            rhs_scale=w_scales[head][:, g, :],
-                            start=(g == 0),
-                            stop=(g == PASSES - 1),
-                        )
-                    nc.vector.tensor_tensor(
-                        out=y[:, a, 0:ROTATED].rearrange("p (b j d) -> p b j d", b=2, d=2),
-                        in0=u[:, 0:ROTATED].rearrange("p (b j d) -> p b j d", b=2, d=2),
-                        in1=cos_tab[:, 0 : i + 2 : i + 1, :].unsqueeze(3).to_broadcast([P, 2, FREQS, 2]),
-                        op=ALU.mult,
-                    )
-                    nc.vector.tensor_tensor(
-                        out=cross[:, a, :].rearrange("p (e j d) -> p e j d", e=2, d=2),
-                        in0=u[:, 0:ROTATED].rearrange("p (j d e) -> p e j d", d=2, e=2),
-                        in1=sin_tab[:, i : blocks : TILES - i, :].unsqueeze(3).to_broadcast([P, 2, FREQS, 2]),
-                        op=ALU.mult,
-                    )
-                    nc.scalar.copy(out=y[:, a, ROTATED:CHANNELS], in_=u[:, ROTATED:CHANNELS])
+        normalise(0)
+        nc.vector.tensor_copy(out=gain_bias[:], in_=gain_bias_ps[:, 0 : 2 * CHUNKS])
+        for i in range(1, TILES):
+            normalise(i)
+        for number in range(W_PIECES):
+            regroup_w_piece(number)
+        quantise_w(0)
+        for group in range(LN_GROUPS):
+            for c in range(CHUNKS):
+                flip(group, c)
+            for g in range(PASSES):
+                quantise_x(group, g)
+        for number in range(W_PIECES, W_LEAD):
+            regroup_w_piece(number)
 
-                    number = head * TILES + i + W_LEAD
-                    if number < HEADS * W_PIECES:
-                        prepare_w_piece(number)
-
-                nc.gpsimd.tensor_tensor(
-                    out=y[:, :, 0:HALF], in0=y[:, :, 0:HALF], in1=cross[:, :, HALF:ROTATED], op=ALU.add
-                )
-                nc.gpsimd.tensor_tensor(
-                    out=y[:, :, HALF:ROTATED], in0=y[:, :, HALF:ROTATED], in1=cross[:, :, 0:HALF], op=ALU.add
-                )
-                nc.sync.dma_start(out=out_head[:, group * GROUP : (group + 1) * GROUP, :], in_=y[:])
+        for number in range(HEADS * GROUPS):
+            head, group = divmod(number, GROUPS)
+            project_group(head, group)
+            rotate_group(head, group)

@@ -33,9 +33,7 @@ CHUNKS = FEATURES // P
 TILES = TOKENS // P
 GROUP = 4
 GROUPS = TILES // GROUP
-LN_GROUP = 2
-LN_GROUPS = TILES // LN_GROUP
-LN_TOKENS = LN_GROUP * P
+GROUP_TOKENS = GROUP * P
 BN_WIDTH = 512
 
 QUARTERS = 4
@@ -61,13 +59,14 @@ def tile_transformerencoderlayer_pa_kernel(tc, x_grid, ln_g, ln_b, w_qk, out_0, 
     with ExitStack() as ctx:
         keep = ctx.enter_context(tc.tile_pool(name="keep", bufs=1))
         small = ctx.enter_context(tc.tile_pool(name="small", bufs=TILES))
-        hat_pool = ctx.enter_context(tc.tile_pool(name="hat", bufs=LN_GROUPS))
+        hat_pool = ctx.enter_context(tc.tile_pool(name="hat", bufs=2))
         stage = ctx.enter_context(tc.tile_pool(name="stage", bufs=2))
         grouped_pool = ctx.enter_context(tc.tile_pool(name="grouped", bufs=2))
         w_pool = ctx.enter_context(tc.tile_pool(name="w", bufs=W_BUFS))
         y_pool = ctx.enter_context(tc.tile_pool(name="y", bufs=5))
         cross_pool = ctx.enter_context(tc.tile_pool(name="cross", bufs=3))
-        psum = ctx.enter_context(tc.psum_pool(name="psum", bufs=8))
+        flip_psum = ctx.enter_context(tc.psum_pool(name="flip", bufs=2))
+        acc_psum = ctx.enter_context(tc.psum_pool(name="acc", bufs=6))
 
         gain_bias_rows = keep.tile([P, P], BF16)
         nc.vector.memset(gain_bias_rows[:], 0.0)
@@ -82,6 +81,7 @@ def tile_transformerencoderlayer_pa_kernel(tc, x_grid, ln_g, ln_b, w_qk, out_0, 
                 nc.sync.dma_start(out=x_sb[:, pair : pair + 2, :], in_=x_view[:, pair : pair + 2, :])
 
         w_view = w_qk.rearrange("(g t p) n -> p g t n", t=PACK, p=P)
+
         w_raw = {}
 
         def load_w(head):
@@ -96,10 +96,6 @@ def tile_transformerencoderlayer_pa_kernel(tc, x_grid, ln_g, ln_b, w_qk, out_0, 
 
         token = keep.tile([P, TILES], I32)
         nc.gpsimd.iota(token[:], pattern=[[1, TILES]], base=0, channel_multiplier=TILES)
-        minus_half = keep.tile([P, 1], F32)
-        nc.gpsimd.memset(minus_half[:], -0.5)
-        ident = keep.tile([P, P], F32)
-        make_identity(nc, ident[:])
 
         freq = keep.tile([P, P], F32)
         ratio = (MAX_FREQ / 2.0) ** (1.0 / (FREQS - 1))
@@ -109,6 +105,92 @@ def tile_transformerencoderlayer_pa_kernel(tc, x_grid, ln_g, ln_b, w_qk, out_0, 
             nc.vector.tensor_scalar_mul(
                 out=freq[:, filled : 2 * filled], in0=freq[:, 0:filled], scalar1=ratio**filled
             )
+
+        minus_half = keep.tile([P, 1], F32)
+        nc.gpsimd.memset(minus_half[:], -0.5)
+        ident = keep.tile([P, P], F32)
+        make_identity(nc, ident[:])
+
+        gain_bias_f32 = keep.tile([P, P], F32)
+        nc.vector.tensor_copy(out=gain_bias_f32[:], in_=gain_bias_rows[:])
+        gain_bias_ps = flip_psum.tile([P, P], F32, tag="flipped")
+        nc.tensor.transpose(gain_bias_ps[:], gain_bias_f32[:], ident[:])
+        gain_bias = keep.tile([P, 2 * CHUNKS], F32)
+        nc.vector.tensor_copy(out=gain_bias[:], in_=gain_bias_ps[:, 0 : 2 * CHUNKS])
+
+        xn_t = keep.tile([P, CHUNKS, TOKENS], BF16)
+        x_codes = keep.tile([P, PASSES, TOKENS], U32, align_bytes=64)
+        x_scales = keep.tile([P, PASSES, TOKENS], U8, align_bytes=64)
+
+        def layer_norm_group(group):
+            group_cols = slice(group * GROUP_TOKENS, (group + 1) * GROUP_TOKENS)
+            x_hat = hat_pool.tile([P, GROUP, FEATURES], F32)
+            for a in range(GROUP):
+                x_tile = x_sb[:, group * GROUP + a, :]
+                stats = small.tile([P, FEATURES // BN_WIDTH, 6], F32)
+                for part in range(FEATURES // BN_WIDTH):
+                    nc.vector.bn_stats(out=stats[:, part, :], in_=x_tile[:, part * BN_WIDTH : (part + 1) * BN_WIDTH])
+                mean_var = small.tile([P, 2], F32)
+                nc.vector.bn_aggr(out=mean_var[:], in_=stats[:].rearrange("p a s -> p (a s)"))
+                neg_mean = small.tile([P, 1], F32)
+                nc.vector.tensor_scalar_mul(out=neg_mean[:], in0=mean_var[:, 0:1], scalar1=-1.0)
+                var_eps = small.tile([P, 1], F32)
+                nc.vector.tensor_scalar_add(out=var_eps[:], in0=mean_var[:, 1:2], scalar1=EPS)
+                rstd = small.tile([P, 1], F32)
+                nc.gpsimd.tensor_tensor(out=rstd[:], in0=var_eps[:], in1=minus_half[:], op=ALU.pow)
+                nc.vector.tensor_scalar(
+                    out=x_hat[:, a, :], in0=x_tile, scalar1=neg_mean[:], scalar2=rstd[:], op0=ALU.add, op1=ALU.mult
+                )
+
+            for c in range(CHUNKS):
+                flipped = flip_psum.tile([P, GROUP, P], F32, tag="flipped")
+                for a in range(GROUP):
+                    nc.tensor.transpose(flipped[:, a, :], x_hat[:, a, c * P : (c + 1) * P], ident[:])
+                nc.scalar.activation(
+                    out=xn_t[:, c, group_cols],
+                    in_=flipped[:].rearrange("p a m -> p (a m)"),
+                    func=ACT.Identity,
+                    scale=gain_bias[:, c : c + 1],
+                    bias=gain_bias[:, CHUNKS + c : CHUNKS + c + 1],
+                )
+
+            for g in range(PASSES):
+                xn_grouped = stage.tile([P, GROUP_TOKENS, PACK], BF16, align_bytes=64)
+                regroup(nc.vector.tensor_copy, xn_grouped[:], xn_t[:, g * PACK : (g + 1) * PACK, group_cols])
+                nc.vector.quantize_mx(
+                    out=x_codes[:, g, group_cols].bitcast(FP8X4),
+                    scales=x_scales[:, g, group_cols],
+                    in_=xn_grouped[:].rearrange("p c t -> p (c t)"),
+                )
+
+        w_grouped = {}
+        w_codes = {}
+        w_scales = {}
+
+        def prepare_w_piece(number):
+            head, piece = divmod(number, W_PIECES)
+            g, quarter = divmod(piece, QUARTERS)
+            piece_cols = slice(quarter * PIECE_CHANNELS, (quarter + 1) * PIECE_CHANNELS)
+            if piece == 0:
+                w_grouped[head] = grouped_pool.tile(
+                    [P, PASSES, CHANNELS, PACK], BF16, align_bytes=64, name="w_grouped"
+                )
+            regroup(nc.scalar.copy, w_grouped[head][:, g, piece_cols, :], w_raw[head][:, g, :, piece_cols])
+            if piece == W_PIECES - 1:
+                w_codes[head] = w_pool.tile([P, PASSES, CHANNELS], U32, align_bytes=64, name="w_codes")
+                w_scales[head] = w_pool.tile([P, PASSES, CHANNELS], U8, align_bytes=64, name="w_scales")
+                nc.vector.quantize_mx(
+                    out=w_codes[head][:].rearrange("p g c -> p (g c)").bitcast(FP8X4),
+                    scales=w_scales[head][:].rearrange("p g c -> p (g c)"),
+                    in_=w_grouped[head][:].rearrange("p g c t -> p (g c t)"),
+                )
+                if head + W_BUFS < HEADS:
+                    load_w(head + W_BUFS)
+
+        layer_norm_group(0)
+        for number in range(W_LEAD):
+            prepare_w_piece(number)
+
         blocks = TILES + 1
         grid_index = keep.tile([P, blocks], I32)
         nc.vector.tensor_single_scalar(out=grid_index[:, 0:TILES], in_=token[:], scalar=GRID - 1, op=ALU.bitwise_and)
@@ -147,163 +229,64 @@ def tile_transformerencoderlayer_pa_kernel(tc, x_grid, ln_g, ln_b, w_qk, out_0, 
             op1=ALU.max,
         )
         two_pi = 2.0 * math.pi
-        sin_tab = keep.tile([P, blocks, FREQS], F32)
         cos_tab = keep.tile([P, blocks, FREQS], F32)
-        nc.scalar.activation(out=sin_tab[:, 0:TILES, :], in_=back[:, 0:TILES, :], func=ACT.Sin, scale=-two_pi)
-        nc.scalar.activation(out=sin_tab[:, TILES:blocks, :], in_=back[:, TILES:blocks, :], func=ACT.Sin, scale=two_pi)
+        sin_tab = keep.tile([P, blocks, FREQS], F32)
         nc.scalar.activation(
             out=cos_tab[:, 1:blocks, :], in_=dist[:, 0:TILES, :], func=ACT.Sin, scale=-two_pi, bias=math.pi / 2.0
         )
         nc.scalar.activation(
             out=cos_tab[:, 0:1, :], in_=dist[:, TILES:blocks, :], func=ACT.Sin, scale=-two_pi, bias=math.pi / 2.0
         )
+        nc.scalar.activation(out=sin_tab[:, 0:TILES, :], in_=back[:, 0:TILES, :], func=ACT.Sin, scale=-two_pi)
+        nc.scalar.activation(out=sin_tab[:, TILES:blocks, :], in_=back[:, TILES:blocks, :], func=ACT.Sin, scale=two_pi)
 
-        gain_bias_f32 = keep.tile([P, P], F32)
-        nc.vector.tensor_copy(out=gain_bias_f32[:], in_=gain_bias_rows[:])
-        gain_bias_ps = psum.tile([P, P], F32, tag="bank")
-        nc.tensor.transpose(gain_bias_ps[:], gain_bias_f32[:], ident[:])
-        gain_bias = keep.tile([P, 2 * CHUNKS], F32)
+        layer_norm_group(1)
 
-        x_hat = {}
-        xn_t = keep.tile([P, CHUNKS, TOKENS], BF16)
-        x_codes = keep.tile([P, PASSES, TOKENS], U32, align_bytes=64)
-        x_scales = keep.tile([P, PASSES, TOKENS], U8, align_bytes=64)
-
-        def normalise(i):
-            group, a = divmod(i, LN_GROUP)
-            if a == 0:
-                x_hat[group] = hat_pool.tile([P, LN_GROUP, FEATURES], F32, name="x_hat")
-            x_tile = x_sb[:, i, :]
-            stats = small.tile([P, FEATURES // BN_WIDTH, 6], F32)
-            for part in range(FEATURES // BN_WIDTH):
-                nc.vector.bn_stats(out=stats[:, part, :], in_=x_tile[:, part * BN_WIDTH : (part + 1) * BN_WIDTH])
-            mean_var = small.tile([P, 2], F32)
-            nc.vector.bn_aggr(out=mean_var[:], in_=stats[:].rearrange("p a s -> p (a s)"))
-            neg_mean = small.tile([P, 1], F32)
-            nc.vector.tensor_scalar_mul(out=neg_mean[:], in0=mean_var[:, 0:1], scalar1=-1.0)
-            var_eps = small.tile([P, 1], F32)
-            nc.vector.tensor_scalar_add(out=var_eps[:], in0=mean_var[:, 1:2], scalar1=EPS)
-            rstd = small.tile([P, 1], F32)
-            nc.gpsimd.tensor_tensor(out=rstd[:], in0=var_eps[:], in1=minus_half[:], op=ALU.pow)
-            nc.gpsimd.tensor_scalar(
-                out=x_hat[group][:, a, :], in0=x_tile, scalar1=neg_mean[:], scalar2=rstd[:], op0=ALU.add, op1=ALU.mult
-            )
-
-        def flip(group, c):
-            flipped = psum.tile([P, LN_GROUP, P], F32, tag="bank")
-            for a in range(LN_GROUP):
-                nc.tensor.transpose(flipped[:, a, :], x_hat[group][:, a, c * P : (c + 1) * P], ident[:])
-            nc.scalar.activation(
-                out=xn_t[:, c, group * LN_TOKENS : (group + 1) * LN_TOKENS],
-                in_=flipped[:].rearrange("p a m -> p (a m)"),
-                func=ACT.Identity,
-                scale=gain_bias[:, c : c + 1],
-                bias=gain_bias[:, CHUNKS + c : CHUNKS + c + 1],
-            )
-
-        def quantise_x(group, g):
-            group_cols = slice(group * LN_TOKENS, (group + 1) * LN_TOKENS)
-            xn_grouped = stage.tile([P, LN_TOKENS, PACK], BF16, align_bytes=64)
-            regroup(nc.vector.tensor_copy, xn_grouped[:], xn_t[:, g * PACK : (g + 1) * PACK, group_cols])
-            nc.vector.quantize_mx(
-                out=x_codes[:, g, group_cols].bitcast(FP8X4),
-                scales=x_scales[:, g, group_cols],
-                in_=xn_grouped[:].rearrange("p c t -> p (c t)"),
-            )
-
-        w_grouped = {}
-        w_codes = {}
-        w_scales = {}
-
-        def regroup_w_piece(number):
-            head, piece = divmod(number, W_PIECES)
-            g, quarter = divmod(piece, QUARTERS)
-            piece_cols = slice(quarter * PIECE_CHANNELS, (quarter + 1) * PIECE_CHANNELS)
-            if piece == 0:
-                w_grouped[head] = grouped_pool.tile(
-                    [P, PASSES, CHANNELS, PACK], BF16, align_bytes=64, name="w_grouped"
-                )
-            regroup(nc.scalar.copy, w_grouped[head][:, g, piece_cols, :], w_raw[head][:, g, :, piece_cols])
-            if piece == W_PIECES - 1 and head + W_BUFS < HEADS:
-                load_w(head + W_BUFS)
-
-        def quantise_w(head):
-            w_codes[head] = w_pool.tile([P, PASSES, CHANNELS], U32, align_bytes=64, name="w_codes")
-            w_scales[head] = w_pool.tile([P, PASSES, CHANNELS], U8, align_bytes=64, name="w_scales")
-            nc.vector.quantize_mx(
-                out=w_codes[head][:].rearrange("p g c -> p (g c)").bitcast(FP8X4),
-                scales=w_scales[head][:].rearrange("p g c -> p (g c)"),
-                in_=w_grouped[head][:].rearrange("p g c t -> p (g c t)"),
-            )
-
-        u_banks = {}
-
-        def project_group(head, group):
-            for i in range(group * GROUP, (group + 1) * GROUP):
-                tile_cols = slice(i * P, (i + 1) * P)
-                u_banks[(head, i)] = psum.tile([P, CHANNELS], F32, tag="bank", name="u")
-                for g in range(PASSES):
-                    nc.tensor.matmul_mx(
-                        out=u_banks[(head, i)][:],
-                        lhsT=x_codes[:, g, tile_cols].bitcast(FP8X4),
-                        lhsT_scale=x_scales[:, g, tile_cols],
-                        rhs=w_codes[head][:, g, :].bitcast(FP8X4),
-                        rhs_scale=w_scales[head][:, g, :],
-                        start=(g == 0),
-                        stop=(g == PASSES - 1),
-                    )
-
-        def rotate_group(head, group):
-            y = y_pool.tile([P, GROUP, CHANNELS], F32)
-            cross = cross_pool.tile([P, GROUP, ROTATED], F32)
-            for a in range(GROUP):
-                i = group * GROUP + a
-                u = u_banks[(head, i)]
-                step = head * TILES + i
-                if step + W_LEAD < HEADS * W_PIECES:
-                    regroup_w_piece(step + W_LEAD)
-                nc.vector.tensor_tensor(
-                    out=y[:, a, 0:ROTATED].rearrange("p (b j d) -> p b j d", b=2, d=2),
-                    in0=u[:, 0:ROTATED].rearrange("p (b j d) -> p b j d", b=2, d=2),
-                    in1=cos_tab[:, 0 : i + 2 : i + 1, :].unsqueeze(3).to_broadcast([P, 2, FREQS, 2]),
-                    op=ALU.mult,
-                )
-                nc.vector.tensor_tensor(
-                    out=cross[:, a, :].rearrange("p (e j d) -> p e j d", e=2, d=2),
-                    in0=u[:, 0:ROTATED].rearrange("p (j d e) -> p e j d", d=2, e=2),
-                    in1=sin_tab[:, i : blocks : TILES - i, :].unsqueeze(3).to_broadcast([P, 2, FREQS, 2]),
-                    op=ALU.mult,
-                )
-                nc.scalar.copy(out=y[:, a, ROTATED:CHANNELS], in_=u[:, ROTATED:CHANNELS])
-                if (step + W_LEAD) % W_PIECES == 0 and step + W_LEAD <= HEADS * W_PIECES:
-                    quantise_w((step + W_LEAD) // W_PIECES - 1)
-
-            last = head == HEADS - 1 and group == GROUPS - 1
-            adder = nc.vector if last else nc.gpsimd
-            adder.tensor_tensor(out=y[:, :, 0:HALF], in0=y[:, :, 0:HALF], in1=cross[:, :, HALF:ROTATED], op=ALU.add)
-            adder.tensor_tensor(
-                out=y[:, :, HALF:ROTATED], in0=y[:, :, HALF:ROTATED], in1=cross[:, :, 0:HALF], op=ALU.add
-            )
+        for head in range(HEADS):
             out_tensor = out_0 if head < HEADS_PER_OUTPUT else out_1
             out_head = out_tensor[0, head % HEADS_PER_OUTPUT].rearrange("(p i) c -> p i c", i=TILES)
-            nc.sync.dma_start(out=out_head[:, group * GROUP : (group + 1) * GROUP, :], in_=y[:])
 
-        normalise(0)
-        nc.vector.tensor_copy(out=gain_bias[:], in_=gain_bias_ps[:, 0 : 2 * CHUNKS])
-        for i in range(1, TILES):
-            normalise(i)
-        for number in range(W_PIECES):
-            regroup_w_piece(number)
-        quantise_w(0)
-        for group in range(LN_GROUPS):
-            for c in range(CHUNKS):
-                flip(group, c)
-            for g in range(PASSES):
-                quantise_x(group, g)
-        for number in range(W_PIECES, W_LEAD):
-            regroup_w_piece(number)
+            for group in range(GROUPS):
+                y = y_pool.tile([P, GROUP, CHANNELS], F32)
+                cross = cross_pool.tile([P, GROUP, ROTATED], F32)
+                for a in range(GROUP):
+                    i = group * GROUP + a
+                    tile_cols = slice(i * P, (i + 1) * P)
+                    u = acc_psum.tile([P, CHANNELS], F32)
+                    for g in range(PASSES):
+                        nc.tensor.matmul_mx(
+                            out=u[:],
+                            lhsT=x_codes[:, g, tile_cols].bitcast(FP8X4),
+                            lhsT_scale=x_scales[:, g, tile_cols],
+                            rhs=w_codes[head][:, g, :].bitcast(FP8X4),
+                            rhs_scale=w_scales[head][:, g, :],
+                            start=(g == 0),
+                            stop=(g == PASSES - 1),
+                        )
+                    nc.vector.tensor_tensor(
+                        out=y[:, a, 0:ROTATED].rearrange("p (b j d) -> p b j d", b=2, d=2),
+                        in0=u[:, 0:ROTATED].rearrange("p (b j d) -> p b j d", b=2, d=2),
+                        in1=cos_tab[:, 0 : i + 2 : i + 1, :].unsqueeze(3).to_broadcast([P, 2, FREQS, 2]),
+                        op=ALU.mult,
+                    )
+                    nc.vector.tensor_tensor(
+                        out=cross[:, a, :].rearrange("p (e j d) -> p e j d", e=2, d=2),
+                        in0=u[:, 0:ROTATED].rearrange("p (j d e) -> p e j d", d=2, e=2),
+                        in1=sin_tab[:, i : blocks : TILES - i, :].unsqueeze(3).to_broadcast([P, 2, FREQS, 2]),
+                        op=ALU.mult,
+                    )
+                    nc.scalar.copy(out=y[:, a, ROTATED:CHANNELS], in_=u[:, ROTATED:CHANNELS])
 
-        for number in range(HEADS * GROUPS):
-            head, group = divmod(number, GROUPS)
-            project_group(head, group)
-            rotate_group(head, group)
+                    number = head * TILES + i + W_LEAD
+                    if number < HEADS * W_PIECES:
+                        prepare_w_piece(number)
+
+                last = head == HEADS - 1 and group == GROUPS - 1
+                adder = nc.vector if last else nc.gpsimd
+                adder.tensor_tensor(
+                    out=y[:, :, 0:HALF], in0=y[:, :, 0:HALF], in1=cross[:, :, HALF:ROTATED], op=ALU.add
+                )
+                adder.tensor_tensor(
+                    out=y[:, :, HALF:ROTATED], in0=y[:, :, HALF:ROTATED], in1=cross[:, :, 0:HALF], op=ALU.add
+                )
+                nc.sync.dma_start(out=out_head[:, group * GROUP : (group + 1) * GROUP, :], in_=y[:])

import math
from contextlib import ExitStack

import concourse.mybir as mybir
from concourse.masks import make_identity

F32 = mybir.dt.float32
BF16 = mybir.dt.bfloat16
I32 = mybir.dt.int32
U32 = mybir.dt.uint32
U8 = mybir.dt.uint8
FP8X4 = mybir.dt.float8_e4m3fn_x4
ALU = mybir.AluOpType
ACT = mybir.ActivationFunctionType

P = 128
GRID = 32
TOKENS = GRID * GRID
FEATURES = 1024
HEADS = 8
HEADS_PER_OUTPUT = 4
CHANNELS = 512
FREQS = 100
HALF = 2 * FREQS
ROTATED = 2 * HALF
MAX_FREQ = 10.0
EPS = 1e-5

PACK = 4
K_PASS = P * PACK
PASSES = FEATURES // K_PASS
CHUNKS = FEATURES // P
TILES = TOKENS // P
GROUP = 4
GROUPS = TILES // GROUP
GROUP_TOKENS = GROUP * P
BN_WIDTH = 512

QUARTERS = 4
PIECE_CHANNELS = CHANNELS // QUARTERS
W_PIECES = PASSES * QUARTERS
W_LEAD = W_PIECES + 2
W_BUFS = 3

ROUND_MAGIC = 12582912.0

FLOPS = 2 * TOKENS * FEATURES * HEADS * CHANNELS


def regroup(copy, grouped, planes):
    copy(
        out=grouped.rearrange("p (c i) t -> p c t i", i=4),
        in_=planes.rearrange("p t (c i) -> p c t i", i=4),
    )


def tile_transformerencoderlayer_pa_kernel(tc, x_grid, ln_g, ln_b, w_qk, out_0, out_1):
    nc = tc.nc
    with ExitStack() as ctx:
        keep = ctx.enter_context(tc.tile_pool(name="keep", bufs=1))
        small = ctx.enter_context(tc.tile_pool(name="small", bufs=TILES))
        hat_pool = ctx.enter_context(tc.tile_pool(name="hat", bufs=2))
        stage = ctx.enter_context(tc.tile_pool(name="stage", bufs=2))
        grouped_pool = ctx.enter_context(tc.tile_pool(name="grouped", bufs=2))
        w_pool = ctx.enter_context(tc.tile_pool(name="w", bufs=W_BUFS))
        y_pool = ctx.enter_context(tc.tile_pool(name="y", bufs=5))
        cross_pool = ctx.enter_context(tc.tile_pool(name="cross", bufs=3))
        flip_psum = ctx.enter_context(tc.psum_pool(name="flip", bufs=2))
        acc_psum = ctx.enter_context(tc.psum_pool(name="acc", bufs=6))

        gain_bias_rows = keep.tile([P, P], BF16)
        nc.vector.memset(gain_bias_rows[:], 0.0)
        nc.sync.dma_start(out=gain_bias_rows[0:CHUNKS, :], in_=ln_g.rearrange("(c p) -> c p", p=P))
        nc.sync.dma_start(out=gain_bias_rows[CHUNKS : 2 * CHUNKS, :], in_=ln_b.rearrange("(c p) -> c p", p=P))

        x_sb = keep.tile([P, TILES, FEATURES], BF16)
        x_view = x_grid[0].rearrange("(p i) d -> p i d", i=TILES)

        def load_x(group):
            for pair in range(group * GROUP, (group + 1) * GROUP, 2):
                nc.sync.dma_start(out=x_sb[:, pair : pair + 2, :], in_=x_view[:, pair : pair + 2, :])

        w_view = w_qk.rearrange("(g t p) n -> p g t n", t=PACK, p=P)

        w_raw = {}

        def load_w(head):
            w_raw[head] = w_pool.tile([P, PASSES, PACK, CHANNELS], BF16, name="w_raw")
            nc.sync.dma_start(out=w_raw[head][:], in_=w_view[:, :, :, head * CHANNELS : (head + 1) * CHANNELS])

        load_x(0)
        load_w(0)
        load_x(1)
        for head in range(1, W_BUFS):
            load_w(head)

        token = keep.tile([P, TILES], I32)
        nc.gpsimd.iota(token[:], pattern=[[1, TILES]], base=0, channel_multiplier=TILES)

        freq = keep.tile([P, P], F32)
        ratio = (MAX_FREQ / 2.0) ** (1.0 / (FREQS - 1))
        nc.vector.memset(freq[:, 0:1], 0.5)
        for doubling in range(7):
            filled = 2**doubling
            nc.vector.tensor_scalar_mul(
                out=freq[:, filled : 2 * filled], in0=freq[:, 0:filled], scalar1=ratio**filled
            )

        minus_half = keep.tile([P, 1], F32)
        nc.gpsimd.memset(minus_half[:], -0.5)
        ident = keep.tile([P, P], F32)
        make_identity(nc, ident[:])

        gain_bias_f32 = keep.tile([P, P], F32)
        nc.vector.tensor_copy(out=gain_bias_f32[:], in_=gain_bias_rows[:])
        gain_bias_ps = flip_psum.tile([P, P], F32, tag="flipped")
        nc.tensor.transpose(gain_bias_ps[:], gain_bias_f32[:], ident[:])
        gain_bias = keep.tile([P, 2 * CHUNKS], F32)
        nc.vector.tensor_copy(out=gain_bias[:], in_=gain_bias_ps[:, 0 : 2 * CHUNKS])

        xn_t = keep.tile([P, CHUNKS, TOKENS], BF16)
        x_codes = keep.tile([P, PASSES, TOKENS], U32, align_bytes=64)
        x_scales = keep.tile([P, PASSES, TOKENS], U8, align_bytes=64)

        def layer_norm_group(group):
            group_cols = slice(group * GROUP_TOKENS, (group + 1) * GROUP_TOKENS)
            x_hat = hat_pool.tile([P, GROUP, FEATURES], F32)
            for a in range(GROUP):
                x_tile = x_sb[:, group * GROUP + a, :]
                stats = small.tile([P, FEATURES // BN_WIDTH, 6], F32)
                for part in range(FEATURES // BN_WIDTH):
                    nc.vector.bn_stats(out=stats[:, part, :], in_=x_tile[:, part * BN_WIDTH : (part + 1) * BN_WIDTH])
                mean_var = small.tile([P, 2], F32)
                nc.vector.bn_aggr(out=mean_var[:], in_=stats[:].rearrange("p a s -> p (a s)"))
                neg_mean = small.tile([P, 1], F32)
                nc.vector.tensor_scalar_mul(out=neg_mean[:], in0=mean_var[:, 0:1], scalar1=-1.0)
                var_eps = small.tile([P, 1], F32)
                nc.vector.tensor_scalar_add(out=var_eps[:], in0=mean_var[:, 1:2], scalar1=EPS)
                rstd = small.tile([P, 1], F32)
                nc.gpsimd.tensor_tensor(out=rstd[:], in0=var_eps[:], in1=minus_half[:], op=ALU.pow)
                nc.vector.tensor_scalar(
                    out=x_hat[:, a, :], in0=x_tile, scalar1=neg_mean[:], scalar2=rstd[:], op0=ALU.add, op1=ALU.mult
                )

            for c in range(CHUNKS):
                flipped = flip_psum.tile([P, GROUP, P], F32, tag="flipped")
                for a in range(GROUP):
                    nc.tensor.transpose(flipped[:, a, :], x_hat[:, a, c * P : (c + 1) * P], ident[:])
                nc.scalar.activation(
                    out=xn_t[:, c, group_cols],
                    in_=flipped[:].rearrange("p a m -> p (a m)"),
                    func=ACT.Identity,
                    scale=gain_bias[:, c : c + 1],
                    bias=gain_bias[:, CHUNKS + c : CHUNKS + c + 1],
                )

            for g in range(PASSES):
                xn_grouped = stage.tile([P, GROUP_TOKENS, PACK], BF16, align_bytes=64)
                regroup(nc.vector.tensor_copy, xn_grouped[:], xn_t[:, g * PACK : (g + 1) * PACK, group_cols])
                nc.vector.quantize_mx(
                    out=x_codes[:, g, group_cols].bitcast(FP8X4),
                    scales=x_scales[:, g, group_cols],
                    in_=xn_grouped[:].rearrange("p c t -> p (c t)"),
                )

        w_grouped = {}
        w_codes = {}
        w_scales = {}

        def prepare_w_piece(number):
            head, piece = divmod(number, W_PIECES)
            g, quarter = divmod(piece, QUARTERS)
            piece_cols = slice(quarter * PIECE_CHANNELS, (quarter + 1) * PIECE_CHANNELS)
            if piece == 0:
                w_grouped[head] = grouped_pool.tile(
                    [P, PASSES, CHANNELS, PACK], BF16, align_bytes=64, name="w_grouped"
                )
            regroup(nc.scalar.copy, w_grouped[head][:, g, piece_cols, :], w_raw[head][:, g, :, piece_cols])
            if piece == W_PIECES - 1:
                w_codes[head] = w_pool.tile([P, PASSES, CHANNELS], U32, align_bytes=64, name="w_codes")
                w_scales[head] = w_pool.tile([P, PASSES, CHANNELS], U8, align_bytes=64, name="w_scales")
                nc.vector.quantize_mx(
                    out=w_codes[head][:].rearrange("p g c -> p (g c)").bitcast(FP8X4),
                    scales=w_scales[head][:].rearrange("p g c -> p (g c)"),
                    in_=w_grouped[head][:].rearrange("p g c t -> p (g c t)"),
                )
                if head + W_BUFS < HEADS:
                    load_w(head + W_BUFS)

        layer_norm_group(0)
        for number in range(W_LEAD):
            prepare_w_piece(number)

        blocks = TILES + 1
        grid_index = keep.tile([P, blocks], I32)
        nc.vector.tensor_single_scalar(out=grid_index[:, 0:TILES], in_=token[:], scalar=GRID - 1, op=ALU.bitwise_and)
        nc.vector.tensor_single_scalar(
            out=grid_index[:, TILES:blocks], in_=token[:, 0:1], scalar=5, op=ALU.arith_shift_right
        )
        coord = keep.tile([P, blocks], F32)
        nc.vector.tensor_scalar(
            out=coord[:], in0=grid_index[:], scalar1=2.0 / (GRID - 1), scalar2=-1.0, op0=ALU.mult, op1=ALU.add
        )
        turn = keep.tile([P, blocks, FREQS], F32)
        nc.vector.tensor_tensor(
            out=turn[:],
            in0=freq[:, 0:FREQS].unsqueeze(1).to_broadcast([P, blocks, FREQS]),
            in1=coord[:].unsqueeze(2).to_broadcast([P, blocks, FREQS]),
            op=ALU.mult,
        )
        rounded = keep.tile([P, blocks, FREQS], F32)
        nc.vector.tensor_scalar_add(out=rounded[:], in0=turn[:], scalar1=ROUND_MAGIC)
        back = keep.tile([P, blocks, FREQS], F32)
        nc.vector.scalar_tensor_tensor(
            out=back[:].rearrange("p b j -> p (b j)"),
            in0=rounded[:].rearrange("p b j -> p (b j)"),
            scalar=ROUND_MAGIC,
            in1=turn[:].rearrange("p b j -> p (b j)"),
            op0=ALU.subtract,
            op1=ALU.subtract,
        )
        dist = keep.tile([P, blocks, FREQS], F32)
        nc.vector.scalar_tensor_tensor(
            out=dist[:].rearrange("p b j -> p (b j)"),
            in0=back[:].rearrange("p b j -> p (b j)"),
            scalar=-1.0,
            in1=back[:].rearrange("p b j -> p (b j)"),
            op0=ALU.mult,
            op1=ALU.max,
        )
        two_pi = 2.0 * math.pi
        cos_tab = keep.tile([P, blocks, FREQS], F32)
        sin_tab = keep.tile([P, blocks, FREQS], F32)
        nc.scalar.activation(
            out=cos_tab[:, 1:blocks, :], in_=dist[:, 0:TILES, :], func=ACT.Sin, scale=-two_pi, bias=math.pi / 2.0
        )
        nc.scalar.activation(
            out=cos_tab[:, 0:1, :], in_=dist[:, TILES:blocks, :], func=ACT.Sin, scale=-two_pi, bias=math.pi / 2.0
        )
        nc.scalar.activation(out=sin_tab[:, 0:TILES, :], in_=back[:, 0:TILES, :], func=ACT.Sin, scale=-two_pi)
        nc.scalar.activation(out=sin_tab[:, TILES:blocks, :], in_=back[:, TILES:blocks, :], func=ACT.Sin, scale=two_pi)

        layer_norm_group(1)

        for head in range(HEADS):
            out_tensor = out_0 if head < HEADS_PER_OUTPUT else out_1
            out_head = out_tensor[0, head % HEADS_PER_OUTPUT].rearrange("(p i) c -> p i c", i=TILES)

            for group in range(GROUPS):
                y = y_pool.tile([P, GROUP, CHANNELS], F32)
                cross = cross_pool.tile([P, GROUP, ROTATED], F32)
                for a in range(GROUP):
                    i = group * GROUP + a
                    tile_cols = slice(i * P, (i + 1) * P)
                    u = acc_psum.tile([P, CHANNELS], F32)
                    for g in range(PASSES):
                        nc.tensor.matmul_mx(
                            out=u[:],
                            lhsT=x_codes[:, g, tile_cols].bitcast(FP8X4),
                            lhsT_scale=x_scales[:, g, tile_cols],
                            rhs=w_codes[head][:, g, :].bitcast(FP8X4),
                            rhs_scale=w_scales[head][:, g, :],
                            start=(g == 0),
                            stop=(g == PASSES - 1),
                        )
                    nc.vector.tensor_tensor(
                        out=y[:, a, 0:ROTATED].rearrange("p (b j d) -> p b j d", b=2, d=2),
                        in0=u[:, 0:ROTATED].rearrange("p (b j d) -> p b j d", b=2, d=2),
                        in1=cos_tab[:, 0 : i + 2 : i + 1, :].unsqueeze(3).to_broadcast([P, 2, FREQS, 2]),
                        op=ALU.mult,
                    )
                    nc.vector.tensor_tensor(
                        out=cross[:, a, :].rearrange("p (e j d) -> p e j d", e=2, d=2),
                        in0=u[:, 0:ROTATED].rearrange("p (j d e) -> p e j d", d=2, e=2),
                        in1=sin_tab[:, i : blocks : TILES - i, :].unsqueeze(3).to_broadcast([P, 2, FREQS, 2]),
                        op=ALU.mult,
                    )
                    nc.scalar.copy(out=y[:, a, ROTATED:CHANNELS], in_=u[:, ROTATED:CHANNELS])

                    number = head * TILES + i + W_LEAD
                    if number < HEADS * W_PIECES:
                        prepare_w_piece(number)

                last = head == HEADS - 1 and group == GROUPS - 1
                adder = nc.vector if last else nc.gpsimd
                adder.tensor_tensor(
                    out=y[:, :, 0:HALF], in0=y[:, :, 0:HALF], in1=cross[:, :, HALF:ROTATED], op=ALU.add
                )
                adder.tensor_tensor(
                    out=y[:, :, HALF:ROTATED], in0=y[:, :, HALF:ROTATED], in1=cross[:, :, 0:HALF], op=ALU.add
                )
                nc.sync.dma_start(out=out_head[:, group * GROUP : (group + 1) * GROUP, :], in_=y[:])
